import numpy as np
import ml_dtypes

BF16 = ml_dtypes.bfloat16


def bf(x):
    return np.asarray(x, np.float32).astype(BF16)


def f32(x):
    return np.asarray(x, np.float32)


def f64(x):
    return np.asarray(x).astype(np.float64)


def striped(idx):
    return np.tile(idx.reshape(-1, 16).T, (8, 1))


S, D, M, N = 1024, 128, 512, 128
ALPHA_Q = 0.3


def elu(v):
    return np.maximum(v, 0.0) + np.exp(np.minimum(v, 0.0)) - 1.0


def sigmoid(v):
    return 1.0 / (1.0 + np.exp(-v))


def setup_inputs():
    return {
        "table": bf(np.random.standard_normal((S, D))),
        "w_i": bf(np.random.standard_normal((D, M)) / np.sqrt(2.0 * D)),
        "w_u": bf(np.random.standard_normal((D, M)) / np.sqrt(2.0 * D)),
        "user_pre": f32(np.random.standard_normal((D, N))),
        "gate_pre": f32(np.random.standard_normal((D, N))),
        "qproj": f32(np.random.standard_normal((D, N))),
        "b1": f32(0.1 * np.random.standard_normal((M, 1))),
        "offs": striped(np.random.permutation(np.tile(np.arange(S), 2))[:N]),
    }


def reference(table, w_i, w_u, user_pre, gate_pre, qproj, b1, offs):
    idx = offs[:16].T.reshape(-1)
    u = elu(f64(user_pre)) + ALPHA_Q * sigmoid(f64(gate_pre)) * f64(qproj)
    acc = f64(w_i).T @ f64(table)[idx].T + f64(w_u).T @ u + f64(b1)
    return np.maximum(acc, 0.0)

@@ -1,0 +1,102 @@
+import concourse.mybir as mybir
+from concourse.masks import make_identity
+
+BF16, F32, U16 = mybir.dt.bfloat16, mybir.dt.float32, mybir.dt.uint16
+ALU = mybir.AluOpType
+FUNC = mybir.ActivationFunctionType
+
+P = 128
+ITEMS, FEATURES, HIDDEN, PAIRS = 1024, 128, 512, 128
+PIECES = 4
+PIECE_ITEMS = ITEMS // PIECES
+ROWS = PIECE_ITEMS // P
+HIDDEN_BLOCKS = HIDDEN // P
+GATE_WEIGHT = 0.3
+
+FLOPS = 2 * (2 * FEATURES) * HIDDEN * PAIRS
+
+
+def tile_bilevelgat_kernel(tc, table, w_i, w_u, user_pre, gate_pre, qproj, b1, offs, out):
+    nc = tc.nc
+    with (
+        tc.tile_pool(name="held", bufs=1) as held,
+        tc.psum_pool(name="psum", bufs=PIECES) as psum,
+    ):
+        table_pieces = table.rearrange("(c p r) k -> c p r k", c=PIECES, p=P)
+        items_first = [held.tile([P, ROWS, FEATURES], BF16, name=f"items_first{c}") for c in range(PIECES)]
+        user = held.tile([P, PAIRS], F32, name="user")
+        gate = held.tile([P, PAIRS], F32, name="gate")
+        gated_term = held.tile([P, PAIRS], F32, name="gated_term")
+        nc.sync.dma_start(items_first[0][:], table_pieces[0])
+        nc.scalar.dma_start(items_first[1][:], table_pieces[1])
+        nc.sync.dma_start(user[:], user_pre)
+        nc.scalar.dma_start(gate[:], gate_pre)
+        nc.sync.dma_start(gated_term[:], qproj)
+        nc.scalar.dma_start(items_first[2][:], table_pieces[2])
+        nc.sync.dma_start(items_first[3][:], table_pieces[3])
+
+        user_weights = held.tile([P, HIDDEN], BF16, name="user_weights")
+        item_weights = held.tile([P, HIDDEN], BF16, name="item_weights")
+        nc.scalar.dma_start(user_weights[:], w_u)
+
+        offsets = held.tile([P, PAIRS // 16], U16, name="offsets")
+        nc.sync.dma_start(item_weights[:, : HIDDEN // 2], w_i[:, : HIDDEN // 2])
+        nc.sync.dma_start(offsets[:], offs)
+        nc.sync.dma_start(item_weights[:, HIDDEN // 2 :], w_i[:, HIDDEN // 2 :])
+
+        bias = held.tile([P, HIDDEN_BLOCKS], F32, name="bias")
+        with nc.allow_non_contiguous_dma(reason="512 floats, one to a partition and block"):
+            nc.sync.dma_start(bias[:], b1.rearrange("(a p) one -> p (a one)", p=P))
+
+        identity = held.tile([P, P], BF16, name="identity")
+        nc.vector.memset(identity[:], 0.0)
+        make_identity(nc, identity[:], nomemset=True)
+
+        window = held.tile([P, ITEMS], BF16, name="window")
+        for c in range(PIECES):
+            features_first = psum.tile([P, ROWS, P], BF16, name=f"features_first{c}", tag="bank")
+            for r in range(ROWS):
+                nc.tensor.transpose(features_first[:, r, :], items_first[c][:, r, :], identity[:])
+            in_table_order = features_first[:].rearrange("k r p -> k p r")
+            piece_of_window = window[:, c * PIECE_ITEMS : (c + 1) * PIECE_ITEMS].rearrange("k (p r) -> k p r", r=ROWS)
+            if c % 2 == 0:
+                nc.scalar.copy(piece_of_window, in_table_order)
+            else:
+                nc.vector.tensor_copy(piece_of_window, in_table_order)
+
+        negative = held.tile([P, PAIRS], F32, name="negative")
+        nc.vector.tensor_scalar_min(negative[:], user[:], 0.0)
+        decay = held.tile([P, PAIRS], F32, name="decay")
+        nc.scalar.activation(decay[:], negative[:], FUNC.Exp)
+        tanh_half = held.tile([P, PAIRS], F32, name="tanh_half")
+        nc.scalar.activation(tanh_half[:], gate[:], FUNC.Tanh, scale=0.5)
+        positive = held.tile([P, PAIRS], F32, name="positive")
+        nc.vector.tensor_scalar(positive[:], user[:], 0.0, -1.0, ALU.max, ALU.add)
+        twice_gated = held.tile([P, PAIRS], F32, name="twice_gated")
+        nc.vector.scalar_tensor_tensor(twice_gated[:], tanh_half[:], 1.0, gated_term[:], ALU.add, ALU.mult)
+        elu = held.tile([P, PAIRS], F32, name="elu")
+        nc.vector.tensor_tensor(elu[:], positive[:], decay[:], ALU.add)
+        u = held.tile([P, PAIRS], BF16, name="u")
+        nc.vector.scalar_tensor_tensor(u[:], twice_gated[:], GATE_WEIGHT / 2, elu[:], ALU.mult, ALU.add)
+
+        banks = [psum.tile([P, PAIRS], F32, name=f"bank{a}", tag="bank") for a in range(HIDDEN_BLOCKS)]
+        for a in range(HIDDEN_BLOCKS):
+            nc.tensor.matmul(banks[a][:], user_weights[:, a * P : (a + 1) * P], u[:], start=True, stop=False)
+        for a in range(HIDDEN_BLOCKS):
+            nc.tensor.matmul(
+                banks[a][:],
+                item_weights[:, a * P : (a + 1) * P],
+                window[:].indirect(offsets[:]),
+                start=False,
+                stop=True,
+            )
+
+        result = held.tile([P, HIDDEN_BLOCKS, PAIRS], F32, name="result")
+        out_blocks = out.rearrange("(a p) j -> p a j", p=P)
+        for a in range(HIDDEN_BLOCKS):
+            if a % 2 == 0:
+                nc.scalar.activation(result[:, a, :], banks[a][:], FUNC.Relu, bias=bias[:, a : a + 1])
+                nc.scalar.dma_start(out_blocks[:, a, :], result[:, a, :])
+            else:
+                nc.vector.tensor_scalar(result[:, a, :], banks[a][:], bias[:, a : a + 1], 0.0, ALU.add, ALU.max)
+                nc.sync.dma_start(out_blocks[:, a, :], result[:, a, :])

@@ -64,10 +64,8 @@ def tile_bilevelgat_kernel(tc, table, w_i, w_u, user_pre, gate_pre, qproj, b1, o
             else:
                 nc.vector.tensor_copy(piece_of_window, in_table_order)
 
-        negative = held.tile([P, PAIRS], F32, name="negative")
-        nc.vector.tensor_scalar_min(negative[:], user[:], 0.0)
-        decay = held.tile([P, PAIRS], F32, name="decay")
-        nc.scalar.activation(decay[:], negative[:], FUNC.Exp)
+        growth = held.tile([P, PAIRS], F32, name="growth")
+        nc.scalar.activation(growth[:], user[:], FUNC.Exp)
         tanh_half = held.tile([P, PAIRS], F32, name="tanh_half")
         nc.scalar.activation(tanh_half[:], gate[:], FUNC.Tanh, scale=0.5)
         positive = held.tile([P, PAIRS], F32, name="positive")
@@ -75,7 +73,7 @@ def tile_bilevelgat_kernel(tc, table, w_i, w_u, user_pre, gate_pre, qproj, b1, o
         twice_gated = held.tile([P, PAIRS], F32, name="twice_gated")
         nc.vector.scalar_tensor_tensor(twice_gated[:], tanh_half[:], 1.0, gated_term[:], ALU.add, ALU.mult)
         elu = held.tile([P, PAIRS], F32, name="elu")
-        nc.vector.tensor_tensor(elu[:], positive[:], decay[:], ALU.add)
+        nc.vector.scalar_tensor_tensor(elu[:], growth[:], 1.0, positive[:], ALU.min, ALU.add)
         u = held.tile([P, PAIRS], BF16, name="u")
         nc.vector.scalar_tensor_tensor(u[:], twice_gated[:], GATE_WEIGHT / 2, elu[:], ALU.mult, ALU.add)
 

import concourse.mybir as mybir
from concourse.masks import make_identity

BF16, F32, U16 = mybir.dt.bfloat16, mybir.dt.float32, mybir.dt.uint16
ALU = mybir.AluOpType
FUNC = mybir.ActivationFunctionType

P = 128
ITEMS, FEATURES, HIDDEN, PAIRS = 1024, 128, 512, 128
PIECES = 4
PIECE_ITEMS = ITEMS // PIECES
ROWS = PIECE_ITEMS // P
HIDDEN_BLOCKS = HIDDEN // P
GATE_WEIGHT = 0.3

FLOPS = 2 * (2 * FEATURES) * HIDDEN * PAIRS


def tile_bilevelgat_kernel(tc, table, w_i, w_u, user_pre, gate_pre, qproj, b1, offs, out):
    nc = tc.nc
    with (
        tc.tile_pool(name="held", bufs=1) as held,
        tc.psum_pool(name="psum", bufs=PIECES) as psum,
    ):
        table_pieces = table.rearrange("(c p r) k -> c p r k", c=PIECES, p=P)
        items_first = [held.tile([P, ROWS, FEATURES], BF16, name=f"items_first{c}") for c in range(PIECES)]
        user = held.tile([P, PAIRS], F32, name="user")
        gate = held.tile([P, PAIRS], F32, name="gate")
        gated_term = held.tile([P, PAIRS], F32, name="gated_term")
        nc.sync.dma_start(items_first[0][:], table_pieces[0])
        nc.scalar.dma_start(items_first[1][:], table_pieces[1])
        nc.sync.dma_start(user[:], user_pre)
        nc.scalar.dma_start(gate[:], gate_pre)
        nc.sync.dma_start(gated_term[:], qproj)
        nc.scalar.dma_start(items_first[2][:], table_pieces[2])
        nc.sync.dma_start(items_first[3][:], table_pieces[3])

        user_weights = held.tile([P, HIDDEN], BF16, name="user_weights")
        item_weights = held.tile([P, HIDDEN], BF16, name="item_weights")
        nc.scalar.dma_start(user_weights[:], w_u)

        offsets = held.tile([P, PAIRS // 16], U16, name="offsets")
        nc.sync.dma_start(item_weights[:, : HIDDEN // 2], w_i[:, : HIDDEN // 2])
        nc.sync.dma_start(offsets[:], offs)
        nc.sync.dma_start(item_weights[:, HIDDEN // 2 :], w_i[:, HIDDEN // 2 :])

        bias = held.tile([P, HIDDEN_BLOCKS], F32, name="bias")
        with nc.allow_non_contiguous_dma(reason="512 floats, one to a partition and block"):
            nc.sync.dma_start(bias[:], b1.rearrange("(a p) one -> p (a one)", p=P))

        identity = held.tile([P, P], BF16, name="identity")
        nc.vector.memset(identity[:], 0.0)
        make_identity(nc, identity[:], nomemset=True)

        window = held.tile([P, ITEMS], BF16, name="window")
        for c in range(PIECES):
            features_first = psum.tile([P, ROWS, P], BF16, name=f"features_first{c}", tag="bank")
            for r in range(ROWS):
                nc.tensor.transpose(features_first[:, r, :], items_first[c][:, r, :], identity[:])
            in_table_order = features_first[:].rearrange("k r p -> k p r")
            piece_of_window = window[:, c * PIECE_ITEMS : (c + 1) * PIECE_ITEMS].rearrange("k (p r) -> k p r", r=ROWS)
            if c % 2 == 0:
                nc.scalar.copy(piece_of_window, in_table_order)
            else:
                nc.vector.tensor_copy(piece_of_window, in_table_order)

        growth = held.tile([P, PAIRS], F32, name="growth")
        nc.scalar.activation(growth[:], user[:], FUNC.Exp)
        tanh_half = held.tile([P, PAIRS], F32, name="tanh_half")
        nc.scalar.activation(tanh_half[:], gate[:], FUNC.Tanh, scale=0.5)
        positive = held.tile([P, PAIRS], F32, name="positive")
        nc.vector.tensor_scalar(positive[:], user[:], 0.0, -1.0, ALU.max, ALU.add)
        twice_gated = held.tile([P, PAIRS], F32, name="twice_gated")
        nc.vector.scalar_tensor_tensor(twice_gated[:], tanh_half[:], 1.0, gated_term[:], ALU.add, ALU.mult)
        elu = held.tile([P, PAIRS], F32, name="elu")
        nc.vector.scalar_tensor_tensor(elu[:], growth[:], 1.0, positive[:], ALU.min, ALU.add)
        u = held.tile([P, PAIRS], BF16, name="u")
        nc.vector.scalar_tensor_tensor(u[:], twice_gated[:], GATE_WEIGHT / 2, elu[:], ALU.mult, ALU.add)

        banks = [psum.tile([P, PAIRS], F32, name=f"bank{a}", tag="bank") for a in range(HIDDEN_BLOCKS)]
        for a in range(HIDDEN_BLOCKS):
            nc.tensor.matmul(banks[a][:], user_weights[:, a * P : (a + 1) * P], u[:], start=True, stop=False)
        for a in range(HIDDEN_BLOCKS):
            nc.tensor.matmul(
                banks[a][:],
                item_weights[:, a * P : (a + 1) * P],
                window[:].indirect(offsets[:]),
                start=False,
                stop=True,
            )

        result = held.tile([P, HIDDEN_BLOCKS, PAIRS], F32, name="result")
        out_blocks = out.rearrange("(a p) j -> p a j", p=P)
        for a in range(HIDDEN_BLOCKS):
            if a % 2 == 0:
                nc.scalar.activation(result[:, a, :], banks[a][:], FUNC.Relu, bias=bias[:, a : a + 1])
                nc.scalar.dma_start(out_blocks[:, a, :], result[:, a, :])
            else:
                nc.vector.tensor_scalar(result[:, a, :], banks[a][:], bias[:, a : a + 1], 0.0, ALU.add, ALU.max)
                nc.sync.dma_start(out_blocks[:, a, :], result[:, a, :])
